import numpy as np
import ml_dtypes


def mxq(x, axis, fmt="e4m3"):
    dtype, down = {"e4m3": (ml_dtypes.float8_e4m3fn, 7), "e5m2": (ml_dtypes.float8_e5m2, 14)}[fmt]
    v = np.moveaxis(np.asarray(x, np.float32).astype(ml_dtypes.bfloat16).astype(np.float64), axis, -1)
    blocks = v.reshape(v.shape[:-1] + (-1, 32))
    amax = np.abs(blocks).max(-1, keepdims=True)
    byte = np.maximum(np.where(amax > 0, np.frexp(amax)[1] - 1 + 127, 0) - down, 1)
    scale = np.exp2(byte - 127.0)
    codes = (blocks / scale).astype(np.float32).astype(dtype).astype(np.float64)
    return np.moveaxis((codes * scale).reshape(v.shape), -1, axis)


WIDE = False


def mx_kscale(k):
    if not WIDE:
        return np.ones(k)
    levels = np.array([10, -10, 5, -5, 0])
    a = np.random.permutation(np.resize(levels, k // 512 * 4)).reshape(k // 512, 4)
    idx = np.arange(k)
    return np.exp2(a[idx // 512, idx % 128 // 32])


BF16 = ml_dtypes.bfloat16


def bf(x):
    return np.asarray(x, np.float32).astype(BF16)


def f64(x):
    return np.asarray(x).astype(np.float64)


E2M1 = np.array([0.0, 0.5, 1.0, 1.5, 2.0, 3.0, 4.0, 6.0, -0.0, -0.5, -1.0, -1.5, -2.0, -3.0, -4.0, -6.0])


def pack_weight(w, fmt):
    k, n = w.shape
    w = f64(bf(w)).reshape(k // 32, 32, n)
    amax = np.abs(w).max(1)
    if fmt == "e4m3":
        byte = np.frexp(amax)[1] - 1 + 127 - 7
    else:
        mant, ex = np.frexp(amax / 6.0)
        byte = np.where(mant > 0.5, ex, ex - 1) + 127
    byte = np.clip(np.where(amax > 0, byte, 1), 1, 254)
    scaled = (w * np.exp2(127.0 - byte)[:, None, :]).reshape(k, n).astype(np.float32)
    by_word = np.ascontiguousarray(scaled.reshape(k // 512, 128, 4, n).transpose(0, 1, 3, 2))
    if fmt == "e4m3":
        words = by_word.astype(ml_dtypes.float8_e4m3fn).view(np.uint8)
    else:
        c = by_word.astype(ml_dtypes.float4_e2m1fn).view(np.uint8) & 0xF
        words = c[..., 0::2] | (c[..., 1::2] << 4)
    return np.ascontiguousarray(words), np.ascontiguousarray(byte.astype(np.uint8).reshape(k // 512, 16, n))


def unpack_weight(words, scales, fmt):
    g, p, n, _ = words.shape
    if fmt == "e4m3":
        vals = np.ascontiguousarray(words).view(ml_dtypes.float8_e4m3fn).astype(np.float64)
    else:
        nib = np.empty((g, p, n, 4), np.uint8)
        nib[..., 0::2] = words & 0xF
        nib[..., 1::2] = words >> 4
        vals = E2M1[nib]
    vals = vals * np.repeat(np.exp2(scales.astype(np.float64) - 127.0), 8, axis=1)[..., None]
    return vals.transpose(0, 1, 3, 2).reshape(g * 512, n)


B, S, D, H, HS, R = 1, 128, 8192, 16, 64, 32
W = 3 * H * HS
HALF = R // 2
THETA = 10000.0


def rope_tables():
    inv = 1.0 / THETA ** (np.arange(0, R, 2) / R)
    pos = THETA - S + np.arange(S)
    ang = pos[:, None] * inv[None, :]
    return np.cos(ang), np.sin(ang)


def apply_rotary(t, cos, sin):
    re, im = t[..., :HALF], t[..., HALF:]
    c, sn = cos[None, :, None, :], sin[None, :, None, :]
    out = np.stack((re * c - im * sn, re * sn + im * c), axis=-1)
    return out.reshape(t.shape)


def setup_inputs():
    s = mx_kscale(D)
    cos, sin = rope_tables()
    x = bf(np.random.standard_normal((B, S, D)) * s)
    words, scales = pack_weight(np.random.standard_normal((D, W)) / np.sqrt(D) / s[:, None], "e4m3")
    b_qkv = bf(np.random.standard_normal(W) * 0.3)
    return {"x": x,
            "w_qkv_words": words, "w_qkv_scales": scales,
            "b_qkv": b_qkv,
            "cos": bf(cos), "sin": bf(sin)}


def reference(x, w_qkv_words, w_qkv_scales, b_qkv, cos, sin):
    cos, sin = f64(cos), f64(sin)
    qkv = (mxq(f64(x), 2, "e4m3") @ unpack_weight(w_qkv_words, w_qkv_scales, "e4m3")) + f64(b_qkv)
    qkv = qkv.reshape(B, S, H, 3 * HS)
    q, k, v = qkv[..., :HS], qkv[..., HS:2 * HS], qkv[..., 2 * HS:]
    q_rot = np.concatenate((apply_rotary(q[..., :R], cos, sin), q[..., R:]), axis=3)
    k_rot = np.concatenate((apply_rotary(k[..., :R], cos, sin), k[..., R:]), axis=3)
    return q_rot, k_rot, v

@@ -1,0 +1,213 @@
+from contextlib import ExitStack
+
+import concourse.mybir as mybir
+from concourse.masks import make_identity
+
+F32 = mybir.dt.float32
+BF16 = mybir.dt.bfloat16
+I32 = mybir.dt.int32
+U32 = mybir.dt.uint32
+U8 = mybir.dt.uint8
+FP8X4 = mybir.dt.float8_e4m3fn_x4
+ADD = mybir.AluOpType.add
+MULT = mybir.AluOpType.mult
+
+P = 128
+TOKENS = 128
+D_MODEL = 8192
+HEADS = 16
+SECTION = 64
+PARTS = 3
+VALUE = 2
+HALF = 16
+WIDTH = PARTS * HEADS * SECTION
+
+PACK = 4
+K_PASS = P * PACK
+PASSES = D_MODEL // K_PASS
+WORDS_PASS = K_PASS // 2
+
+BANK = 512
+BANKS = WIDTH // BANK
+SECTIONS_BANK = BANK // SECTION
+FIRST_BANKS = BANKS - 1
+FIRST_COLS = FIRST_BANKS * BANK
+
+PLANES_TILE = 4
+LAST_CHUNK = 4
+X_PIECES = 4
+W_BUFS = 10
+
+FLOPS = 2 * TOKENS * D_MODEL * WIDTH
+
+
+def sections_of(part, bank):
+    start = SECTIONS_BANK * bank
+    return range(start + (part - start) % PARTS, start + SECTIONS_BANK, PARTS)
+
+
+def heads_before(part, bank):
+    return len(range(part, SECTIONS_BANK * bank, PARTS))
+
+
+def tile_gptneoxattention_pa_k_kernel(
+    tc, x, w_qkv_words, w_qkv_scales, b_qkv, cos, sin, out_0, out_1, out_2
+):
+    nc = tc.nc
+    outs = (out_0, out_1, out_2)
+    with ExitStack() as ctx:
+        keep = ctx.enter_context(tc.tile_pool(name="keep", bufs=1))
+        stream = ctx.enter_context(tc.tile_pool(name="stream", bufs=W_BUFS))
+        work = ctx.enter_context(tc.tile_pool(name="work", bufs=2))
+        psum = ctx.enter_context(tc.psum_pool(name="psum", bufs=8))
+
+        planes = keep.tile([P, PASSES // PLANES_TILE, WIDTH], U8, align_bytes=64)
+        nc.vector.memset(planes[:].bitcast(I32), 0)
+
+        x_sb = keep.tile([P, D_MODEL], BF16)
+        piece = D_MODEL // X_PIECES
+        for c in range(X_PIECES):
+            nc.sync.dma_start(
+                out=x_sb[:, piece * c : piece * (c + 1)], in_=x[0, :, piece * c : piece * (c + 1)]
+            )
+        for slab in range(PASSES // PLANES_TILE):
+            for quad in range(4):
+                nc.sync.dma_start(
+                    out=planes[32 * quad : 32 * quad + 16, slab, :].bitcast(I32),
+                    in_=w_qkv_scales[
+                        PLANES_TILE * slab : PLANES_TILE * (slab + 1), 4 * quad : 4 * quad + 4, :
+                    ].bitcast(I32),
+                )
+
+        bias_rows = keep.tile([P, WIDTH], BF16)
+        nc.vector.memset(bias_rows[:].bitcast(I32), 0)
+        nc.scalar.dma_start(out=bias_rows[0:1, :], in_=b_qkv.unsqueeze(0))
+        cos_sb = keep.tile([P, HALF], BF16)
+        sin_sb = keep.tile([P, HALF], BF16)
+        nc.scalar.dma_start(out=cos_sb[:], in_=cos)
+        nc.scalar.dma_start(out=sin_sb[:], in_=sin)
+
+        ones = keep.tile([P, P], BF16)
+        nc.vector.memset(ones[:], 1.0)
+        bias = keep.tile([P, WIDTH], F32)
+        for b in range(BANKS):
+            spread = psum.tile([P, BANK], F32, tag="bank")
+            nc.tensor.matmul(
+                out=spread[:],
+                lhsT=ones[:],
+                rhs=bias_rows[:, BANK * b : BANK * (b + 1)],
+                start=True,
+                stop=True,
+            )
+            nc.scalar.copy(out=bias[:, BANK * b : BANK * (b + 1)], in_=spread[:])
+
+        by_re = keep.tile([P, HALF, 2], F32)
+        by_im = keep.tile([P, HALF, 2], F32)
+        nc.vector.tensor_copy(out=by_re[:, :, 0], in_=cos_sb[:])
+        nc.vector.tensor_copy(out=by_re[:, :, 1], in_=sin_sb[:])
+        nc.vector.tensor_scalar(out=by_im[:, :, 0], in0=sin_sb[:], scalar1=-1.0, scalar2=None, op0=MULT)
+        nc.vector.tensor_copy(out=by_im[:, :, 1], in_=cos_sb[:])
+
+        ident = keep.tile([P, P], F32)
+        make_identity(nc, ident[:])
+        x_words = x_sb[:].bitcast(F32)
+        grouped = keep.tile([P, PASSES * TOKENS * PACK], BF16, align_bytes=64)
+        x_codes = keep.tile([P, PASSES * TOKENS], U32, align_bytes=64)
+        x_scales = keep.tile([P, PASSES * TOKENS], U8, align_bytes=64)
+        for i in range(PASSES // 2):
+            flipped = psum.tile([P, 2, 2, TOKENS], F32, tag="bank")
+            for s in range(2):
+                first_word = WORDS_PASS * (2 * i + s)
+                for u in range(2):
+                    nc.tensor.transpose(
+                        flipped[:, s, u, :],
+                        x_words[:, first_word + u : first_word + WORDS_PASS : 2],
+                        ident[:],
+                    )
+            values = slice(2 * TOKENS * PACK * i, 2 * TOKENS * PACK * (i + 1))
+            words = slice(2 * TOKENS * i, 2 * TOKENS * (i + 1))
+            copy_out = nc.vector.tensor_copy if i % 2 == 0 else nc.scalar.copy
+            copy_out(
+                out=grouped[:, values].bitcast(F32).rearrange("p (s r u) -> p s r u", s=2, u=2),
+                in_=flipped[:].rearrange("p s u r -> p s r u"),
+            )
+            nc.vector.quantize_mx(
+                out=x_codes[:, words].bitcast(FP8X4), scales=x_scales[:, words], in_=grouped[:, values]
+            )
+
+        acc = [psum.tile([P, BANK], F32, tag="bank", name="acc%d" % b) for b in range(BANKS)]
+
+        def project(g, b, w_words):
+            k0 = PACK * (g % PLANES_TILE)
+            nc.tensor.matmul_mx(
+                out=acc[b][:],
+                lhsT=x_codes[:, TOKENS * g : TOKENS * (g + 1)].bitcast(FP8X4),
+                lhsT_scale=x_scales[:, TOKENS * g : TOKENS * (g + 1)],
+                rhs=w_words.bitcast(FP8X4),
+                rhs_scale=planes[k0:P, g // PLANES_TILE, BANK * b : BANK * (b + 1)],
+                start=(g == 0),
+                stop=(g == PASSES - 1),
+            )
+
+        result = keep.tile([P, PARTS, HEADS, SECTION], F32)
+        bias_sections = bias[:].rearrange("p (s f) -> p s f", f=SECTION)
+
+        def finish(b0, b1, queue):
+            for b in range(b0, b1):
+                acc_sections = acc[b][:].rearrange("p (s f) -> p s f", f=SECTION)
+                for part in range(PARTS):
+                    secs = sections_of(part, b)
+                    h = secs[0] // PARTS
+                    nc.vector.tensor_tensor(
+                        out=result[:, part, h : h + len(secs), :],
+                        in0=acc_sections[:, secs[0] - SECTIONS_BANK * b : SECTIONS_BANK : PARTS, :],
+                        in1=bias_sections[:, secs[0] : SECTIONS_BANK * (b + 1) : PARTS, :],
+                        op=ADD,
+                    )
+            for part in (VALUE, 0, 1):
+                h0, h1 = heads_before(part, b0), heads_before(part, b1)
+                if part != VALUE:
+                    shape = [P, h1 - h0, HALF, 2]
+                    from_re = work.tile(shape, F32, tag="from_re")
+                    from_im = work.tile(shape, F32, tag="from_im")
+                    nc.vector.tensor_tensor(
+                        out=from_re[:],
+                        in0=result[:, part, h0:h1, 0:HALF].unsqueeze(3).to_broadcast(shape),
+                        in1=by_re[:].unsqueeze(1).to_broadcast(shape),
+                        op=MULT,
+                    )
+                    nc.vector.tensor_tensor(
+                        out=from_im[:],
+                        in0=result[:, part, h0:h1, HALF : 2 * HALF].unsqueeze(3).to_broadcast(shape),
+                        in1=by_im[:].unsqueeze(1).to_broadcast(shape),
+                        op=MULT,
+                    )
+                    nc.vector.tensor_tensor(
+                        out=result[:, part, h0:h1, 0 : 2 * HALF].rearrange("p h (j e) -> p h j e", e=2),
+                        in0=from_re[:],
+                        in1=from_im[:],
+                        op=ADD,
+                    )
+                queue.dma_start(out=outs[part][0, :, h0:h1, :], in_=result[:, part, h0:h1, :])
+
+        for g in range(PASSES):
+            w_first = stream.tile([P, PACK * FIRST_COLS], U8, tag="w", align_bytes=64)
+            nc.sync.dma_start(
+                out=w_first[:].bitcast(I32),
+                in_=w_qkv_words[g, :, 0:FIRST_COLS, :].rearrange("p n t -> p (n t)").bitcast(I32),
+            )
+            for b in range(FIRST_BANKS):
+                project(g, b, w_first[:, PACK * BANK * b : PACK * BANK * (b + 1)])
+        finish(0, FIRST_BANKS, nc.scalar)
+
+        for g0 in range(0, PASSES, LAST_CHUNK):
+            w_last = stream.tile([P, LAST_CHUNK, PACK * BANK], U8, tag="w", align_bytes=64)
+            nc.sync.dma_start(
+                out=w_last[:].bitcast(I32),
+                in_=w_qkv_words[g0 : g0 + LAST_CHUNK, :, FIRST_COLS:WIDTH, :]
+                .rearrange("g p n t -> p g (n t)")
+                .bitcast(I32),
+            )
+            for s in range(LAST_CHUNK):
+                project(g0 + s, FIRST_BANKS, w_last[:, s, :])
+        finish(FIRST_BANKS, BANKS, nc.sync)

@@ -64,20 +64,21 @@ def tile_gptneoxattention_pa_k_kernel(
         planes = keep.tile([P, PASSES // PLANES_TILE, WIDTH], U8, align_bytes=64)
         nc.vector.memset(planes[:].bitcast(I32), 0)
 
+        for slab in range(PASSES // PLANES_TILE):
+            for quad in range(4):
+                nc.gpsimd.dma_start(
+                    out=planes[32 * quad : 32 * quad + 16, slab, :].bitcast(F32),
+                    in_=w_qkv_scales[
+                        PLANES_TILE * slab : PLANES_TILE * (slab + 1), 4 * quad : 4 * quad + 4, :
+                    ].bitcast(F32),
+                )
+
         x_sb = keep.tile([P, D_MODEL], BF16)
         piece = D_MODEL // X_PIECES
         for c in range(X_PIECES):
             nc.sync.dma_start(
                 out=x_sb[:, piece * c : piece * (c + 1)], in_=x[0, :, piece * c : piece * (c + 1)]
             )
-        for slab in range(PASSES // PLANES_TILE):
-            for quad in range(4):
-                nc.sync.dma_start(
-                    out=planes[32 * quad : 32 * quad + 16, slab, :].bitcast(I32),
-                    in_=w_qkv_scales[
-                        PLANES_TILE * slab : PLANES_TILE * (slab + 1), 4 * quad : 4 * quad + 4, :
-                    ].bitcast(I32),
-                )
 
         bias_rows = keep.tile([P, WIDTH], BF16)
         nc.vector.memset(bias_rows[:].bitcast(I32), 0)

@@ -18,6 +18,7 @@ D_MODEL = 8192
 HEADS = 16
 SECTION = 64
 PARTS = 3
+ROTATED = (0, 1)
 VALUE = 2
 HALF = 16
 WIDTH = PARTS * HEADS * SECTION
@@ -34,7 +35,7 @@ FIRST_BANKS = BANKS - 1
 FIRST_COLS = FIRST_BANKS * BANK
 
 PLANES_TILE = 4
-LAST_CHUNK = 4
+LAST_CHUNK = 5
 X_PIECES = 4
 W_BUFS = 10
 
@@ -64,21 +65,20 @@ def tile_gptneoxattention_pa_k_kernel(
         planes = keep.tile([P, PASSES // PLANES_TILE, WIDTH], U8, align_bytes=64)
         nc.vector.memset(planes[:].bitcast(I32), 0)
 
-        for slab in range(PASSES // PLANES_TILE):
-            for quad in range(4):
-                nc.gpsimd.dma_start(
-                    out=planes[32 * quad : 32 * quad + 16, slab, :].bitcast(F32),
-                    in_=w_qkv_scales[
-                        PLANES_TILE * slab : PLANES_TILE * (slab + 1), 4 * quad : 4 * quad + 4, :
-                    ].bitcast(F32),
-                )
-
         x_sb = keep.tile([P, D_MODEL], BF16)
         piece = D_MODEL // X_PIECES
         for c in range(X_PIECES):
             nc.sync.dma_start(
                 out=x_sb[:, piece * c : piece * (c + 1)], in_=x[0, :, piece * c : piece * (c + 1)]
             )
+        for slab in range(PASSES // PLANES_TILE):
+            for quad in range(4):
+                nc.sync.dma_start(
+                    out=planes[32 * quad : 32 * quad + 16, slab, :].bitcast(I32),
+                    in_=w_qkv_scales[
+                        PLANES_TILE * slab : PLANES_TILE * (slab + 1), 4 * quad : 4 * quad + 4, :
+                    ].bitcast(I32),
+                )
 
         bias_rows = keep.tile([P, WIDTH], BF16)
         nc.vector.memset(bias_rows[:].bitcast(I32), 0)
@@ -153,7 +153,11 @@ def tile_gptneoxattention_pa_k_kernel(
         result = keep.tile([P, PARTS, HEADS, SECTION], F32)
         bias_sections = bias[:].rearrange("p (s f) -> p s f", f=SECTION)
 
-        def finish(b0, b1, queue):
+        def store(part, b0, b1):
+            h0, h1 = heads_before(part, b0), heads_before(part, b1)
+            nc.sync.dma_start(out=outs[part][0, :, h0:h1, :], in_=result[:, part, h0:h1, :])
+
+        def finish(b0, b1):
             for b in range(b0, b1):
                 acc_sections = acc[b][:].rearrange("p (s f) -> p s f", f=SECTION)
                 for part in range(PARTS):
@@ -165,31 +169,29 @@ def tile_gptneoxattention_pa_k_kernel(
                         in1=bias_sections[:, secs[0] : SECTIONS_BANK * (b + 1) : PARTS, :],
                         op=ADD,
                     )
-            for part in (VALUE, 0, 1):
-                h0, h1 = heads_before(part, b0), heads_before(part, b1)
-                if part != VALUE:
+            store(VALUE, b0, b1)
+            products = {}
+            for first, factors in ((0, by_re), (HALF, by_im)):
+                for part in ROTATED:
+                    h0, h1 = heads_before(part, b0), heads_before(part, b1)
                     shape = [P, h1 - h0, HALF, 2]
-                    from_re = work.tile(shape, F32, tag="from_re")
-                    from_im = work.tile(shape, F32, tag="from_im")
+                    product = work.tile(shape, F32, tag="product%d" % first)
                     nc.vector.tensor_tensor(
-                        out=from_re[:],
-                        in0=result[:, part, h0:h1, 0:HALF].unsqueeze(3).to_broadcast(shape),
-                        in1=by_re[:].unsqueeze(1).to_broadcast(shape),
+                        out=product[:],
+                        in0=result[:, part, h0:h1, first : first + HALF].unsqueeze(3).to_broadcast(shape),
+                        in1=factors[:].unsqueeze(1).to_broadcast(shape),
                         op=MULT,
                     )
-                    nc.vector.tensor_tensor(
-                        out=from_im[:],
-                        in0=result[:, part, h0:h1, HALF : 2 * HALF].unsqueeze(3).to_broadcast(shape),
-                        in1=by_im[:].unsqueeze(1).to_broadcast(shape),
-                        op=MULT,
-                    )
-                    nc.vector.tensor_tensor(
-                        out=result[:, part, h0:h1, 0 : 2 * HALF].rearrange("p h (j e) -> p h j e", e=2),
-                        in0=from_re[:],
-                        in1=from_im[:],
-                        op=ADD,
-                    )
-                queue.dma_start(out=outs[part][0, :, h0:h1, :], in_=result[:, part, h0:h1, :])
+                    products[(part, first)] = product
+            for part in ROTATED:
+                h0, h1 = heads_before(part, b0), heads_before(part, b1)
+                nc.vector.tensor_tensor(
+                    out=result[:, part, h0:h1, 0 : 2 * HALF].rearrange("p h (j e) -> p h j e", e=2),
+                    in0=products[(part, 0)][:],
+                    in1=products[(part, HALF)][:],
+                    op=ADD,
+                )
+                store(part, b0, b1)
 
         for g in range(PASSES):
             w_first = stream.tile([P, PACK * FIRST_COLS], U8, tag="w", align_bytes=64)
@@ -199,16 +201,20 @@ def tile_gptneoxattention_pa_k_kernel(
             )
             for b in range(FIRST_BANKS):
                 project(g, b, w_first[:, PACK * BANK * b : PACK * BANK * (b + 1)])
-        finish(0, FIRST_BANKS, nc.scalar)
 
+        last_tiles = []
         for g0 in range(0, PASSES, LAST_CHUNK):
+            n = min(LAST_CHUNK, PASSES - g0)
             w_last = stream.tile([P, LAST_CHUNK, PACK * BANK], U8, tag="w", align_bytes=64)
             nc.sync.dma_start(
-                out=w_last[:].bitcast(I32),
-                in_=w_qkv_words[g0 : g0 + LAST_CHUNK, :, FIRST_COLS:WIDTH, :]
+                out=w_last[:, 0:n, :].bitcast(I32),
+                in_=w_qkv_words[g0 : g0 + n, :, FIRST_COLS:WIDTH, :]
                 .rearrange("g p n t -> p g (n t)")
                 .bitcast(I32),
             )
-            for s in range(LAST_CHUNK):
-                project(g0 + s, FIRST_BANKS, w_last[:, s, :])
-        finish(FIRST_BANKS, BANKS, nc.sync)
+            last_tiles.append(w_last)
+
+        finish(0, FIRST_BANKS)
+        for g in range(PASSES):
+            project(g, FIRST_BANKS, last_tiles[g // LAST_CHUNK][:, g % LAST_CHUNK, :])
+        finish(FIRST_BANKS, BANKS)

@@ -62,8 +62,20 @@ def tile_gptneoxattention_pa_k_kernel(
         work = ctx.enter_context(tc.tile_pool(name="work", bufs=2))
         psum = ctx.enter_context(tc.psum_pool(name="psum", bufs=8))
 
+        ident = keep.tile([P, P], F32)
+        make_identity(nc, ident[:])
+
         planes = keep.tile([P, PASSES // PLANES_TILE, WIDTH], U8, align_bytes=64)
         nc.vector.memset(planes[:].bitcast(I32), 0)
+
+        for slab in range(PASSES // PLANES_TILE):
+            for quad in range(4):
+                nc.gpsimd.dma_start(
+                    out=planes[32 * quad : 32 * quad + 16, slab, :].bitcast(F32),
+                    in_=w_qkv_scales[
+                        PLANES_TILE * slab : PLANES_TILE * (slab + 1), 4 * quad : 4 * quad + 4, :
+                    ].bitcast(F32),
+                )
 
         x_sb = keep.tile([P, D_MODEL], BF16)
         piece = D_MODEL // X_PIECES
@@ -71,14 +83,6 @@ def tile_gptneoxattention_pa_k_kernel(
             nc.sync.dma_start(
                 out=x_sb[:, piece * c : piece * (c + 1)], in_=x[0, :, piece * c : piece * (c + 1)]
             )
-        for slab in range(PASSES // PLANES_TILE):
-            for quad in range(4):
-                nc.sync.dma_start(
-                    out=planes[32 * quad : 32 * quad + 16, slab, :].bitcast(I32),
-                    in_=w_qkv_scales[
-                        PLANES_TILE * slab : PLANES_TILE * (slab + 1), 4 * quad : 4 * quad + 4, :
-                    ].bitcast(I32),
-                )
 
         bias_rows = keep.tile([P, WIDTH], BF16)
         nc.vector.memset(bias_rows[:].bitcast(I32), 0)
@@ -109,8 +113,6 @@ def tile_gptneoxattention_pa_k_kernel(
         nc.vector.tensor_scalar(out=by_im[:, :, 0], in0=sin_sb[:], scalar1=-1.0, scalar2=None, op0=MULT)
         nc.vector.tensor_copy(out=by_im[:, :, 1], in_=cos_sb[:])
 
-        ident = keep.tile([P, P], F32)
-        make_identity(nc, ident[:])
         x_words = x_sb[:].bitcast(F32)
         grouped = keep.tile([P, PASSES * TOKENS * PACK], BF16, align_bytes=64)
         x_codes = keep.tile([P, PASSES * TOKENS], U32, align_bytes=64)

@@ -36,8 +36,9 @@ FIRST_COLS = FIRST_BANKS * BANK
 
 PLANES_TILE = 4
 LAST_CHUNK = 5
-X_PIECES = 4
-W_BUFS = 10
+X_PIECES = 2
+FIRST_CHUNK = 2
+W_BUFS = 6
 
 FLOPS = 2 * TOKENS * D_MODEL * WIDTH
 
@@ -195,14 +196,17 @@ def tile_gptneoxattention_pa_k_kernel(
                 )
                 store(part, b0, b1)
 
-        for g in range(PASSES):
-            w_first = stream.tile([P, PACK * FIRST_COLS], U8, tag="w", align_bytes=64)
+        for g0 in range(0, PASSES, FIRST_CHUNK):
+            w_first = stream.tile([P, FIRST_CHUNK, PACK * FIRST_COLS], U8, tag="w", align_bytes=64)
             nc.sync.dma_start(
                 out=w_first[:].bitcast(I32),
-                in_=w_qkv_words[g, :, 0:FIRST_COLS, :].rearrange("p n t -> p (n t)").bitcast(I32),
+                in_=w_qkv_words[g0 : g0 + FIRST_CHUNK, :, 0:FIRST_COLS, :]
+                .rearrange("g p n t -> p g (n t)")
+                .bitcast(I32),
             )
-            for b in range(FIRST_BANKS):
-                project(g, b, w_first[:, PACK * BANK * b : PACK * BANK * (b + 1)])
+            for s in range(FIRST_CHUNK):
+                for b in range(FIRST_BANKS):
+                    project(g0 + s, b, w_first[:, s, PACK * BANK * b : PACK * BANK * (b + 1)])
 
         last_tiles = []
         for g0 in range(0, PASSES, LAST_CHUNK):

@@ -31,14 +31,13 @@ WORDS_PASS = K_PASS // 2
 BANK = 512
 BANKS = WIDTH // BANK
 SECTIONS_BANK = BANK // SECTION
-FIRST_BANKS = BANKS - 1
-FIRST_COLS = FIRST_BANKS * BANK
+FULL_PASSES = 10
+FULL_CHUNK = 2
+TAIL_RANGES = [(0, 3, (10, 14)), (3, 5, (10, 13, 15)), (5, 6, (10, 15))]
 
 PLANES_TILE = 4
-LAST_CHUNK = 5
 X_PIECES = 2
-FIRST_CHUNK = 2
-W_BUFS = 6
+W_BUFS = 5
 
 FLOPS = 2 * TOKENS * D_MODEL * WIDTH
 
@@ -93,20 +92,6 @@ def tile_gptneoxattention_pa_k_kernel(
         nc.scalar.dma_start(out=cos_sb[:], in_=cos)
         nc.scalar.dma_start(out=sin_sb[:], in_=sin)
 
-        ones = keep.tile([P, P], BF16)
-        nc.vector.memset(ones[:], 1.0)
-        bias = keep.tile([P, WIDTH], F32)
-        for b in range(BANKS):
-            spread = psum.tile([P, BANK], F32, tag="bank")
-            nc.tensor.matmul(
-                out=spread[:],
-                lhsT=ones[:],
-                rhs=bias_rows[:, BANK * b : BANK * (b + 1)],
-                start=True,
-                stop=True,
-            )
-            nc.scalar.copy(out=bias[:, BANK * b : BANK * (b + 1)], in_=spread[:])
-
         by_re = keep.tile([P, HALF, 2], F32)
         by_im = keep.tile([P, HALF, 2], F32)
         nc.vector.tensor_copy(out=by_re[:, :, 0], in_=cos_sb[:])
@@ -139,26 +124,48 @@ def tile_gptneoxattention_pa_k_kernel(
                 out=x_codes[:, words].bitcast(FP8X4), scales=x_scales[:, words], in_=grouped[:, values]
             )
 
+        ones = keep.tile([P, P], BF16)
+        nc.vector.memset(ones[:], 1.0)
+        bias = keep.tile([P, WIDTH], F32)
+        for b in range(BANKS):
+            spread = psum.tile([P, BANK], F32, tag="bank")
+            nc.tensor.matmul(
+                out=spread[:],
+                lhsT=ones[:],
+                rhs=bias_rows[:, BANK * b : BANK * (b + 1)],
+                start=True,
+                stop=True,
+            )
+            nc.scalar.copy(out=bias[:, BANK * b : BANK * (b + 1)], in_=spread[:])
+
         acc = [psum.tile([P, BANK], F32, tag="bank", name="acc%d" % b) for b in range(BANKS)]
 
-        def project(g, b, w_words):
-            k0 = PACK * (g % PLANES_TILE)
-            nc.tensor.matmul_mx(
-                out=acc[b][:],
-                lhsT=x_codes[:, TOKENS * g : TOKENS * (g + 1)].bitcast(FP8X4),
-                lhsT_scale=x_scales[:, TOKENS * g : TOKENS * (g + 1)],
-                rhs=w_words.bitcast(FP8X4),
-                rhs_scale=planes[k0:P, g // PLANES_TILE, BANK * b : BANK * (b + 1)],
-                start=(g == 0),
-                stop=(g == PASSES - 1),
+        def load(b0, b1, g0, g1):
+            w = stream.tile([P, g1 - g0, PACK * BANK * (b1 - b0)], U8, tag="w", align_bytes=64)
+            nc.sync.dma_start(
+                out=w[:].bitcast(I32),
+                in_=w_qkv_words[g0:g1, :, BANK * b0 : BANK * b1, :]
+                .rearrange("g p n t -> p g (n t)")
+                .bitcast(I32),
             )
+            return w
+
+        def project(b0, b1, g0, g1, w):
+            for g in range(g0, g1):
+                k0 = PACK * (g % PLANES_TILE)
+                for b in range(b0, b1):
+                    nc.tensor.matmul_mx(
+                        out=acc[b][:],
+                        lhsT=x_codes[:, TOKENS * g : TOKENS * (g + 1)].bitcast(FP8X4),
+                        lhsT_scale=x_scales[:, TOKENS * g : TOKENS * (g + 1)],
+                        rhs=w[:, g - g0, PACK * BANK * (b - b0) : PACK * BANK * (b - b0 + 1)].bitcast(FP8X4),
+                        rhs_scale=planes[k0:P, g // PLANES_TILE, BANK * b : BANK * (b + 1)],
+                        start=(g == 0),
+                        stop=(g == PASSES - 1),
+                    )
 
         result = keep.tile([P, PARTS, HEADS, SECTION], F32)
         bias_sections = bias[:].rearrange("p (s f) -> p s f", f=SECTION)
-
-        def store(part, b0, b1):
-            h0, h1 = heads_before(part, b0), heads_before(part, b1)
-            nc.sync.dma_start(out=outs[part][0, :, h0:h1, :], in_=result[:, part, h0:h1, :])
 
         def finish(b0, b1):
             for b in range(b0, b1):
@@ -172,7 +179,6 @@ def tile_gptneoxattention_pa_k_kernel(
                         in1=bias_sections[:, secs[0] : SECTIONS_BANK * (b + 1) : PARTS, :],
                         op=ADD,
                     )
-            store(VALUE, b0, b1)
             products = {}
             for first, factors in ((0, by_re), (HALF, by_im)):
                 for part in ROTATED:
@@ -194,33 +200,20 @@ def tile_gptneoxattention_pa_k_kernel(
                     in1=products[(part, HALF)][:],
                     op=ADD,
                 )
-                store(part, b0, b1)
 
-        for g0 in range(0, PASSES, FIRST_CHUNK):
-            w_first = stream.tile([P, FIRST_CHUNK, PACK * FIRST_COLS], U8, tag="w", align_bytes=64)
-            nc.sync.dma_start(
-                out=w_first[:].bitcast(I32),
-                in_=w_qkv_words[g0 : g0 + FIRST_CHUNK, :, 0:FIRST_COLS, :]
-                .rearrange("g p n t -> p g (n t)")
-                .bitcast(I32),
-            )
-            for s in range(FIRST_CHUNK):
-                for b in range(FIRST_BANKS):
-                    project(g0 + s, b, w_first[:, s, PACK * BANK * b : PACK * BANK * (b + 1)])
+        def store(b0, b1):
+            for part in (VALUE,) + ROTATED:
+                h0, h1 = heads_before(part, b0), heads_before(part, b1)
+                nc.sync.dma_start(out=outs[part][0, :, h0:h1, :], in_=result[:, part, h0:h1, :])
 
-        last_tiles = []
-        for g0 in range(0, PASSES, LAST_CHUNK):
-            n = min(LAST_CHUNK, PASSES - g0)
-            w_last = stream.tile([P, LAST_CHUNK, PACK * BANK], U8, tag="w", align_bytes=64)
-            nc.sync.dma_start(
-                out=w_last[:, 0:n, :].bitcast(I32),
-                in_=w_qkv_words[g0 : g0 + n, :, FIRST_COLS:WIDTH, :]
-                .rearrange("g p n t -> p g (n t)")
-                .bitcast(I32),
-            )
-            last_tiles.append(w_last)
-
-        finish(0, FIRST_BANKS)
-        for g in range(PASSES):
-            project(g, FIRST_BANKS, last_tiles[g // LAST_CHUNK][:, g % LAST_CHUNK, :])
-        finish(FIRST_BANKS, BANKS)
+        for g in range(0, FULL_PASSES, FULL_CHUNK):
+            w = load(0, BANKS, g, g + FULL_CHUNK)
+            project(0, BANKS, g, g + FULL_CHUNK, w)
+        for b0, b1, cuts in TAIL_RANGES:
+            for g0, g1 in zip(cuts, cuts[1:] + (PASSES,)):
+                w = load(b0, b1, g0, g1)
+                project(b0, b1, g0, g1, w)
+            if b1 == BANKS:
+                store(0, b0)
+            finish(b0, b1)
+        store(b0, b1)

@@ -31,9 +31,9 @@ WORDS_PASS = K_PASS // 2
 BANK = 512
 BANKS = WIDTH // BANK
 SECTIONS_BANK = BANK // SECTION
-FULL_PASSES = 10
+FULL_PASSES = 11
 FULL_CHUNK = 2
-TAIL_RANGES = [(0, 3, (10, 14)), (3, 5, (10, 13, 15)), (5, 6, (10, 15))]
+TAIL_RANGES = [(0, 3, (11, 14)), (3, 5, (11, 14)), (5, 6, (11, 15))]
 
 PLANES_TILE = 4
 X_PIECES = 2
@@ -61,21 +61,26 @@ def tile_gptneoxattention_pa_k_kernel(
         stream = ctx.enter_context(tc.tile_pool(name="stream", bufs=W_BUFS))
         work = ctx.enter_context(tc.tile_pool(name="work", bufs=2))
         psum = ctx.enter_context(tc.psum_pool(name="psum", bufs=8))
+        ctx.enter_context(tc.manual_schedule(engines={mybir.EngineType.SP}))
 
         ident = keep.tile([P, P], F32)
         make_identity(nc, ident[:])
 
         planes = keep.tile([P, PASSES // PLANES_TILE, WIDTH], U8, align_bytes=64)
-        nc.vector.memset(planes[:].bitcast(I32), 0)
-
         for slab in range(PASSES // PLANES_TILE):
+            nc.vector.memset(planes[:, slab, :].bitcast(I32), 0)
+
+        def load_scales(queue, slab, dtype):
             for quad in range(4):
-                nc.gpsimd.dma_start(
-                    out=planes[32 * quad : 32 * quad + 16, slab, :].bitcast(F32),
+                queue.dma_start(
+                    out=planes[32 * quad : 32 * quad + 16, slab, :].bitcast(dtype),
                     in_=w_qkv_scales[
                         PLANES_TILE * slab : PLANES_TILE * (slab + 1), 4 * quad : 4 * quad + 4, :
-                    ].bitcast(F32),
+                    ].bitcast(dtype),
                 )
+
+        for slab in (2, 3):
+            load_scales(nc.gpsimd, slab, F32)
 
         x_sb = keep.tile([P, D_MODEL], BF16)
         piece = D_MODEL // X_PIECES
@@ -83,6 +88,8 @@ def tile_gptneoxattention_pa_k_kernel(
             nc.sync.dma_start(
                 out=x_sb[:, piece * c : piece * (c + 1)], in_=x[0, :, piece * c : piece * (c + 1)]
             )
+        for slab in (0, 1):
+            load_scales(nc.sync, slab, I32)
 
         bias_rows = keep.tile([P, WIDTH], BF16)
         nc.vector.memset(bias_rows[:].bitcast(I32), 0)
@@ -206,9 +213,10 @@ def tile_gptneoxattention_pa_k_kernel(
                 h0, h1 = heads_before(part, b0), heads_before(part, b1)
                 nc.sync.dma_start(out=outs[part][0, :, h0:h1, :], in_=result[:, part, h0:h1, :])
 
-        for g in range(0, FULL_PASSES, FULL_CHUNK):
-            w = load(0, BANKS, g, g + FULL_CHUNK)
-            project(0, BANKS, g, g + FULL_CHUNK, w)
+        for g0 in range(0, FULL_PASSES, FULL_CHUNK):
+            g1 = min(g0 + FULL_CHUNK, FULL_PASSES)
+            w = load(0, BANKS, g0, g1)
+            project(0, BANKS, g0, g1, w)
         for b0, b1, cuts in TAIL_RANGES:
             for g0, g1 in zip(cuts, cuts[1:] + (PASSES,)):
                 w = load(b0, b1, g0, g1)

@@ -79,7 +79,7 @@ def tile_gptneoxattention_pa_k_kernel(
                     ].bitcast(dtype),
                 )
 
-        for slab in (2, 3):
+        for slab in (1, 2, 3):
             load_scales(nc.gpsimd, slab, F32)
 
         x_sb = keep.tile([P, D_MODEL], BF16)
@@ -88,8 +88,7 @@ def tile_gptneoxattention_pa_k_kernel(
             nc.sync.dma_start(
                 out=x_sb[:, piece * c : piece * (c + 1)], in_=x[0, :, piece * c : piece * (c + 1)]
             )
-        for slab in (0, 1):
-            load_scales(nc.sync, slab, I32)
+        load_scales(nc.sync, 0, I32)
 
         bias_rows = keep.tile([P, WIDTH], BF16)
         nc.vector.memset(bias_rows[:].bitcast(I32), 0)
@@ -222,6 +221,7 @@ def tile_gptneoxattention_pa_k_kernel(
                 w = load(b0, b1, g0, g1)
                 project(b0, b1, g0, g1, w)
             if b1 == BANKS:
-                store(0, b0)
+                for r0, r1, ignored in TAIL_RANGES[:-1]:
+                    store(r0, r1)
             finish(b0, b1)
         store(b0, b1)

from contextlib import ExitStack

import concourse.mybir as mybir
from concourse.masks import make_identity

F32 = mybir.dt.float32
BF16 = mybir.dt.bfloat16
I32 = mybir.dt.int32
U32 = mybir.dt.uint32
U8 = mybir.dt.uint8
FP8X4 = mybir.dt.float8_e4m3fn_x4
ADD = mybir.AluOpType.add
MULT = mybir.AluOpType.mult

P = 128
TOKENS = 128
D_MODEL = 8192
HEADS = 16
SECTION = 64
PARTS = 3
ROTATED = (0, 1)
VALUE = 2
HALF = 16
WIDTH = PARTS * HEADS * SECTION

PACK = 4
K_PASS = P * PACK
PASSES = D_MODEL // K_PASS
WORDS_PASS = K_PASS // 2

BANK = 512
BANKS = WIDTH // BANK
SECTIONS_BANK = BANK // SECTION
FULL_PASSES = 11
FULL_CHUNK = 2
TAIL_RANGES = [(0, 3, (11, 14)), (3, 5, (11, 14)), (5, 6, (11, 15))]

PLANES_TILE = 4
X_PIECES = 2
W_BUFS = 5

FLOPS = 2 * TOKENS * D_MODEL * WIDTH


def sections_of(part, bank):
    start = SECTIONS_BANK * bank
    return range(start + (part - start) % PARTS, start + SECTIONS_BANK, PARTS)


def heads_before(part, bank):
    return len(range(part, SECTIONS_BANK * bank, PARTS))


def tile_gptneoxattention_pa_k_kernel(
    tc, x, w_qkv_words, w_qkv_scales, b_qkv, cos, sin, out_0, out_1, out_2
):
    nc = tc.nc
    outs = (out_0, out_1, out_2)
    with ExitStack() as ctx:
        keep = ctx.enter_context(tc.tile_pool(name="keep", bufs=1))
        stream = ctx.enter_context(tc.tile_pool(name="stream", bufs=W_BUFS))
        work = ctx.enter_context(tc.tile_pool(name="work", bufs=2))
        psum = ctx.enter_context(tc.psum_pool(name="psum", bufs=8))
        ctx.enter_context(tc.manual_schedule(engines={mybir.EngineType.SP}))

        ident = keep.tile([P, P], F32)
        make_identity(nc, ident[:])

        planes = keep.tile([P, PASSES // PLANES_TILE, WIDTH], U8, align_bytes=64)
        for slab in range(PASSES // PLANES_TILE):
            nc.vector.memset(planes[:, slab, :].bitcast(I32), 0)

        def load_scales(queue, slab, dtype):
            for quad in range(4):
                queue.dma_start(
                    out=planes[32 * quad : 32 * quad + 16, slab, :].bitcast(dtype),
                    in_=w_qkv_scales[
                        PLANES_TILE * slab : PLANES_TILE * (slab + 1), 4 * quad : 4 * quad + 4, :
                    ].bitcast(dtype),
                )

        for slab in (1, 2, 3):
            load_scales(nc.gpsimd, slab, F32)

        x_sb = keep.tile([P, D_MODEL], BF16)
        piece = D_MODEL // X_PIECES
        for c in range(X_PIECES):
            nc.sync.dma_start(
                out=x_sb[:, piece * c : piece * (c + 1)], in_=x[0, :, piece * c : piece * (c + 1)]
            )
        load_scales(nc.sync, 0, I32)

        bias_rows = keep.tile([P, WIDTH], BF16)
        nc.vector.memset(bias_rows[:].bitcast(I32), 0)
        nc.scalar.dma_start(out=bias_rows[0:1, :], in_=b_qkv.unsqueeze(0))
        cos_sb = keep.tile([P, HALF], BF16)
        sin_sb = keep.tile([P, HALF], BF16)
        nc.scalar.dma_start(out=cos_sb[:], in_=cos)
        nc.scalar.dma_start(out=sin_sb[:], in_=sin)

        by_re = keep.tile([P, HALF, 2], F32)
        by_im = keep.tile([P, HALF, 2], F32)
        nc.vector.tensor_copy(out=by_re[:, :, 0], in_=cos_sb[:])
        nc.vector.tensor_copy(out=by_re[:, :, 1], in_=sin_sb[:])
        nc.vector.tensor_scalar(out=by_im[:, :, 0], in0=sin_sb[:], scalar1=-1.0, scalar2=None, op0=MULT)
        nc.vector.tensor_copy(out=by_im[:, :, 1], in_=cos_sb[:])

        x_words = x_sb[:].bitcast(F32)
        grouped = keep.tile([P, PASSES * TOKENS * PACK], BF16, align_bytes=64)
        x_codes = keep.tile([P, PASSES * TOKENS], U32, align_bytes=64)
        x_scales = keep.tile([P, PASSES * TOKENS], U8, align_bytes=64)
        for i in range(PASSES // 2):
            flipped = psum.tile([P, 2, 2, TOKENS], F32, tag="bank")
            for s in range(2):
                first_word = WORDS_PASS * (2 * i + s)
                for u in range(2):
                    nc.tensor.transpose(
                        flipped[:, s, u, :],
                        x_words[:, first_word + u : first_word + WORDS_PASS : 2],
                        ident[:],
                    )
            values = slice(2 * TOKENS * PACK * i, 2 * TOKENS * PACK * (i + 1))
            words = slice(2 * TOKENS * i, 2 * TOKENS * (i + 1))
            copy_out = nc.vector.tensor_copy if i % 2 == 0 else nc.scalar.copy
            copy_out(
                out=grouped[:, values].bitcast(F32).rearrange("p (s r u) -> p s r u", s=2, u=2),
                in_=flipped[:].rearrange("p s u r -> p s r u"),
            )
            nc.vector.quantize_mx(
                out=x_codes[:, words].bitcast(FP8X4), scales=x_scales[:, words], in_=grouped[:, values]
            )

        ones = keep.tile([P, P], BF16)
        nc.vector.memset(ones[:], 1.0)
        bias = keep.tile([P, WIDTH], F32)
        for b in range(BANKS):
            spread = psum.tile([P, BANK], F32, tag="bank")
            nc.tensor.matmul(
                out=spread[:],
                lhsT=ones[:],
                rhs=bias_rows[:, BANK * b : BANK * (b + 1)],
                start=True,
                stop=True,
            )
            nc.scalar.copy(out=bias[:, BANK * b : BANK * (b + 1)], in_=spread[:])

        acc = [psum.tile([P, BANK], F32, tag="bank", name="acc%d" % b) for b in range(BANKS)]

        def load(b0, b1, g0, g1):
            w = stream.tile([P, g1 - g0, PACK * BANK * (b1 - b0)], U8, tag="w", align_bytes=64)
            nc.sync.dma_start(
                out=w[:].bitcast(I32),
                in_=w_qkv_words[g0:g1, :, BANK * b0 : BANK * b1, :]
                .rearrange("g p n t -> p g (n t)")
                .bitcast(I32),
            )
            return w

        def project(b0, b1, g0, g1, w):
            for g in range(g0, g1):
                k0 = PACK * (g % PLANES_TILE)
                for b in range(b0, b1):
                    nc.tensor.matmul_mx(
                        out=acc[b][:],
                        lhsT=x_codes[:, TOKENS * g : TOKENS * (g + 1)].bitcast(FP8X4),
                        lhsT_scale=x_scales[:, TOKENS * g : TOKENS * (g + 1)],
                        rhs=w[:, g - g0, PACK * BANK * (b - b0) : PACK * BANK * (b - b0 + 1)].bitcast(FP8X4),
                        rhs_scale=planes[k0:P, g // PLANES_TILE, BANK * b : BANK * (b + 1)],
                        start=(g == 0),
                        stop=(g == PASSES - 1),
                    )

        result = keep.tile([P, PARTS, HEADS, SECTION], F32)
        bias_sections = bias[:].rearrange("p (s f) -> p s f", f=SECTION)

        def finish(b0, b1):
            for b in range(b0, b1):
                acc_sections = acc[b][:].rearrange("p (s f) -> p s f", f=SECTION)
                for part in range(PARTS):
                    secs = sections_of(part, b)
                    h = secs[0] // PARTS
                    nc.vector.tensor_tensor(
                        out=result[:, part, h : h + len(secs), :],
                        in0=acc_sections[:, secs[0] - SECTIONS_BANK * b : SECTIONS_BANK : PARTS, :],
                        in1=bias_sections[:, secs[0] : SECTIONS_BANK * (b + 1) : PARTS, :],
                        op=ADD,
                    )
            products = {}
            for first, factors in ((0, by_re), (HALF, by_im)):
                for part in ROTATED:
                    h0, h1 = heads_before(part, b0), heads_before(part, b1)
                    shape = [P, h1 - h0, HALF, 2]
                    product = work.tile(shape, F32, tag="product%d" % first)
                    nc.vector.tensor_tensor(
                        out=product[:],
                        in0=result[:, part, h0:h1, first : first + HALF].unsqueeze(3).to_broadcast(shape),
                        in1=factors[:].unsqueeze(1).to_broadcast(shape),
                        op=MULT,
                    )
                    products[(part, first)] = product
            for part in ROTATED:
                h0, h1 = heads_before(part, b0), heads_before(part, b1)
                nc.vector.tensor_tensor(
                    out=result[:, part, h0:h1, 0 : 2 * HALF].rearrange("p h (j e) -> p h j e", e=2),
                    in0=products[(part, 0)][:],
                    in1=products[(part, HALF)][:],
                    op=ADD,
                )

        def store(b0, b1):
            for part in (VALUE,) + ROTATED:
                h0, h1 = heads_before(part, b0), heads_before(part, b1)
                nc.sync.dma_start(out=outs[part][0, :, h0:h1, :], in_=result[:, part, h0:h1, :])

        for g0 in range(0, FULL_PASSES, FULL_CHUNK):
            g1 = min(g0 + FULL_CHUNK, FULL_PASSES)
            w = load(0, BANKS, g0, g1)
            project(0, BANKS, g0, g1, w)
        for b0, b1, cuts in TAIL_RANGES:
            for g0, g1 in zip(cuts, cuts[1:] + (PASSES,)):
                w = load(b0, b1, g0, g1)
                project(b0, b1, g0, g1, w)
            if b1 == BANKS:
                for r0, r1, ignored in TAIL_RANGES[:-1]:
                    store(r0, r1)
            finish(b0, b1)
        store(b0, b1)
